import numpy as np
import ml_dtypes


def mxq(x, axis, fmt="e4m3"):
    dtype, down = {"e4m3": (ml_dtypes.float8_e4m3fn, 7), "e5m2": (ml_dtypes.float8_e5m2, 14)}[fmt]
    v = np.moveaxis(np.asarray(x, np.float32).astype(ml_dtypes.bfloat16).astype(np.float64), axis, -1)
    blocks = v.reshape(v.shape[:-1] + (-1, 32))
    amax = np.abs(blocks).max(-1, keepdims=True)
    byte = np.maximum(np.where(amax > 0, np.frexp(amax)[1] - 1 + 127, 0) - down, 1)
    scale = np.exp2(byte - 127.0)
    codes = (blocks / scale).astype(np.float32).astype(dtype).astype(np.float64)
    return np.moveaxis((codes * scale).reshape(v.shape), -1, axis)


WIDE = False


def mx_kscale(k):
    if not WIDE:
        return np.ones(k)
    levels = np.array([10, -10, 5, -5, 0])
    if k % 512:
        return np.exp2(np.random.permutation(np.resize(levels, k // 32))).repeat(32)
    a = np.empty((k // 512, 16))
    for p in range(k // 512):
        a[p, :8] = np.random.permutation(np.resize(levels, 8))
        for g in range(8):
            far = levels[np.abs(levels - a[p, g]) >= 10]
            a[p, g + 8] = far[np.random.randint(len(far))]
    return np.exp2(a.ravel()).repeat(32)


BF16 = ml_dtypes.bfloat16


def bf(x):
    return np.asarray(x, np.float32).astype(BF16)


def f64(x):
    return np.asarray(x).astype(np.float64)


B, L, C, D, H, Q = 2, 1024, 1024, 1024, 8, 256
EPS = 1e-5


def layer_norm(v, w, b):
    mu = v.mean(-1, keepdims=True)
    var = v.var(-1, keepdims=True)
    return (v - mu) * (1.0 / np.sqrt(var + EPS)) * w + b


def setup_inputs():
    s = mx_kscale(C)
    mag = 10.0 ** (-2.5 * np.random.uniform(size=(B, L, 1)))
    x = (np.random.standard_normal((B, L, C)) + 0.5 * np.random.standard_normal((B, L, 1))) * mag
    return {"x": bf(x),
            "ln_k_w": bf((1.0 + 0.1 * np.random.standard_normal(C)) * s),
            "ln_k_b": bf(0.1 * np.random.standard_normal(C) * s),
            "Wk": bf(np.random.standard_normal((D, C)) / np.sqrt(C) / s[None, :]),
            "Wv": bf(np.random.standard_normal((D, C)) / np.sqrt(C) / s[None, :]),
            "bk": bf(0.1 * np.random.standard_normal(D)),
            "bv": bf(0.1 * np.random.standard_normal(D))}


def reference(x, ln_k_w, ln_k_b, Wk, Wv, bk, bv):
    xk = mxq(layer_norm(f64(x), f64(ln_k_w), f64(ln_k_b)), 2, "e4m3")
    k = (xk @ mxq(f64(Wk).T, 0, "e4m3")) + f64(bk)
    v = (xk @ mxq(f64(Wv).T, 0, "e4m3")) + f64(bv)
    return k, v

@@ -1,0 +1,495 @@
+from contextlib import ExitStack
+
+import concourse.mybir as mybir
+from concourse.masks import make_identity
+
+F32 = mybir.dt.float32
+BF16 = mybir.dt.bfloat16
+U32 = mybir.dt.uint32
+U8 = mybir.dt.uint8
+FP8X4 = mybir.dt.float8_e4m3fn_x4
+ALU = mybir.AluOpType
+ACT = mybir.ActivationFunctionType
+
+P = 128
+FEATURES = 1024
+EPS = 1e-5
+TILES = 16
+GROUPS = 8
+CHUNK = 512
+FLOPS = 2 * 2048 * 1024 * 2048
+
+PSUM_RING = 4
+NORMALISED_BUFS = 6
+PLANES_BUFS = 3
+GROUPED_BUFS = 4
+RESULT_BUFS = 5
+
+STATS_ON_VECTOR = tuple(range(10))
+NORMALISE_ON_VECTOR = tuple(range(4))
+REGROUP_1_ON_SCALAR = (0, 2, 6, 7)
+SECOND_PASS = {1: (11,), 2: (12,), 3: (13,), 4: (14, 15)}
+FIRST_PASS = {1: (12,), 2: (13,), 3: (14, 15)}
+
+
+def regroup_engine(j, g):
+    if g == 0:
+        return "V" if j == 0 else "G"
+    return "S" if j in REGROUP_1_ON_SCALAR else "V"
+
+
+def tile_attentionalpoolerwmasking_pa_kernel(tc, x, ln_k_w, ln_k_b, Wk, Wv, bk, bv, out_0, out_1):
+    nc = tc.nc
+    tokens = x.flatten_outer_dims()
+    outs = (out_0.flatten_outer_dims(), out_1.flatten_outer_dims())
+    with ExitStack() as ctx:
+        ctx.enter_context(tc.manual_schedule())
+        keep = ctx.enter_context(tc.tile_pool(name="keep", bufs=1))
+        normalised_pool = ctx.enter_context(tc.tile_pool(name="normalised", bufs=NORMALISED_BUFS))
+        alternating = ctx.enter_context(tc.tile_pool(name="alternating", bufs=2))
+        planes_pool = ctx.enter_context(tc.tile_pool(name="planes", bufs=PLANES_BUFS))
+        grouped_pool = ctx.enter_context(tc.tile_pool(name="grouped", bufs=GROUPED_BUFS))
+        result_pool = ctx.enter_context(tc.tile_pool(name="result", bufs=RESULT_BUFS))
+        transposes_psum = ctx.enter_context(tc.psum_pool(name="transposes", bufs=PSUM_RING))
+        sums_psum = ctx.enter_context(tc.psum_pool(name="sums", bufs=PSUM_RING))
+
+        vector_rows = keep.tile([P, 512], BF16, name="vector_rows")
+        bias_rows = keep.tile([P, 2048], BF16, name="bias_rows")
+        ones = keep.tile([P, P], BF16, name="ones")
+        zero = keep.tile([P, 1], F32, name="zero")
+        eps = keep.tile([P, 1], F32, name="eps")
+        warm = keep.tile([P, 1], F32, name="warm")
+        identity = keep.tile([P, P], F32, name="identity")
+        gain_shift = keep.tile([P, 16], F32, name="gain_shift")
+        bias = keep.tile([P, 2048], BF16, name="bias")
+        x_in = [keep.tile([P, 2, FEATURES], BF16, name="x_in%d" % j) for j in range(GROUPS)]
+        w_in = [keep.tile([P, 4, FEATURES], BF16, name="w_in%d" % c) for c in range(4)]
+        w_codes = keep.tile([P, 2, 2048], U32, name="w_codes", align_bytes=64)
+        w_scales = keep.tile([P, 2, 2048], U8, name="w_scales", align_bytes=64)
+        x_codes = [keep.tile([P, 2, 256], U32, name="x_codes%d" % j, align_bytes=64) for j in range(GROUPS)]
+        x_scales = [keep.tile([P, 2, 256], U8, name="x_scales%d" % j, align_bytes=64) for j in range(GROUPS)]
+        chunk_stats = {i: keep.tile([P, 2, 6], F32, name="chunk_stats%d" % i) for i in STATS_ON_VECTOR}
+        mean_var = {i: keep.tile([P, 2], F32, name="mean_var%d" % i) for i in STATS_ON_VECTOR}
+        x_sum = {i: keep.tile([P, 1], F32, name="x_sum%d" % i) for i in range(TILES) if i not in STATS_ON_VECTOR}
+        sq_sum = {i: keep.tile([P, 1], F32, name="sq_sum%d" % i) for i in range(TILES) if i not in STATS_ON_VECTOR}
+        minus_mean = [keep.tile([P, 1], F32, name="minus_mean%d" % i) for i in range(TILES)]
+        std = [keep.tile([P, 2], F32, name="std%d" % j) for j in range(GROUPS)]
+        rstd = [keep.tile([P, 2], F32, name="rstd%d" % j) for j in range(GROUPS)]
+        live = {}
+
+        def x_tile(i):
+            return x_in[i // 2][:, i % 2, :]
+
+        def constants_vector():
+            nc.vector.memset(vector_rows[:], 0.0)
+            nc.vector.memset(zero[:], 0.0)
+            nc.vector.tensor_scalar(out=eps[:], in0=zero[:], scalar1=EPS, scalar2=None, op0=ALU.add)
+            nc.vector.memset(bias_rows[:], 0.0)
+            nc.vector.memset(ones[:], 1.0)
+
+        def constants_scalar():
+            nc.scalar.activation(out=warm[:], in_=eps[:], func=ACT.Sqrt)
+
+        def constants_gpsimd():
+            make_identity(nc, identity[:])
+
+        def load_gain_shift():
+            nc.scalar.dma_start(out=vector_rows[0:2, :], in_=ln_k_w.rearrange("(v q) -> v q", v=2))
+            nc.scalar.dma_start(out=vector_rows[2:4, :], in_=ln_k_b.rearrange("(v q) -> v q", v=2))
+
+        def load_bias():
+            nc.scalar.dma_start(out=bias_rows[0:1, 0:1024], in_=bk.rearrange("(o d) -> o d", o=1))
+            nc.scalar.dma_start(out=bias_rows[0:1, 1024:2048], in_=bv.rearrange("(o d) -> o d", o=1))
+
+        def load_tokens(j, n0, count):
+            r0 = P * (2 * j + n0)
+            nc.sync.dma_start(
+                out=x_in[j][:, n0 : n0 + count, :],
+                in_=tokens[r0 : r0 + P * count, :].rearrange("(n p) c -> p n c", p=P),
+            )
+
+        def load_weights(c, n0, count):
+            w = Wk if c < 2 else Wv
+            r0 = CHUNK * (c % 2) + P * n0
+            nc.sync.dma_start(
+                out=w_in[c][:, n0 : n0 + count, :], in_=w[r0 : r0 + P * count, :].rearrange("(n p) c -> p n c", p=P)
+            )
+
+        def transpose_gain_shift():
+            bank = transposes_psum.tile([P, CHUNK], F32, tag="bank", name="vector_bank")
+            live["vector_bank"] = bank
+            words = vector_rows[:].bitcast(F32)
+            for u in range(2):
+                nc.tensor.transpose(bank[:, P * u : P * u + P], words[:, u : 256 : 2], identity[:])
+
+        def keep_gain_shift():
+            nc.vector.tensor_copy(
+                out=gain_shift[:].rearrange("p (r u e) -> p r u e", u=2, e=2),
+                in_=live["vector_bank"][:, 0:256].bitcast(BF16).rearrange("p (u r e) -> p r u e", u=2, e=2)[:, 0:4, :, :],
+            )
+
+        def spread_bias(h):
+            bank = transposes_psum.tile([P, 1024], BF16, tag="bank", name="bias_bank")
+            live[("bias_bank", h)] = bank
+            for c in range(2):
+                o = 1024 * h + CHUNK * c
+                nc.tensor.matmul(
+                    out=bank[:, CHUNK * c : CHUNK * c + CHUNK], lhsT=ones[:], rhs=bias_rows[:, o : o + CHUNK],
+                    start=True, stop=True,
+                )
+
+        def keep_bias(h):
+            nc.scalar.copy(out=bias[:, 1024 * h : 1024 * h + 1024], in_=live[("bias_bank", h)][:])
+
+        def transpose_weights(c, n):
+            bank = transposes_psum.tile([P, CHUNK], F32, tag="bank", name="weight_bank")
+            live[("weight_bank", c, n)] = bank
+            words = w_in[c][:, n, :].bitcast(F32)
+            for g in range(2):
+                for u in range(2):
+                    o = 256 * g + P * u
+                    nc.tensor.transpose(bank[:, o : o + P], words[:, 256 * g + u : 256 * g + 256 : 2], identity[:])
+
+        def regroup_weights(c, n):
+            if ("weight_pairs", c) not in live:
+                live[("weight_pairs", c)] = alternating.tile(
+                    [P, 2, 2048], BF16, tag="weight_pairs", name="weight_pairs", align_bytes=64
+                )
+            words = live[("weight_pairs", c)][:].bitcast(F32).rearrange("p g (d u) -> p g d u", u=2)
+            nc.scalar.copy(
+                out=words[:, :, P * n : P * n + P, :],
+                in_=live[("weight_bank", c, n)][:].rearrange("p (g u d) -> p g d u", g=2, u=2),
+            )
+
+        def quantise_weights(c, g):
+            nc.vector.quantize_mx(
+                out=w_codes[:, g, CHUNK * c : CHUNK * c + CHUNK].bitcast(FP8X4),
+                scales=w_scales[:, g, CHUNK * c : CHUNK * c + CHUNK],
+                in_=live[("weight_pairs", c)][:, g, :],
+            )
+
+        def stats_vector(i):
+            for h in range(2):
+                nc.vector.bn_stats(out=chunk_stats[i][:, h, :], in_=x_tile(i)[:, 512 * h : 512 * h + 512])
+
+        def mean_var_vector(i):
+            nc.vector.bn_aggr(out=mean_var[i][:], in_=chunk_stats[i][:].rearrange("p a b -> p (a b)"))
+
+        def negate_mean(i):
+            eng = nc.vector if i in NORMALISE_ON_VECTOR else nc.gpsimd
+            eng.tensor_scalar(
+                out=minus_mean[i][:], in0=mean_var[i][:, 0:1], scalar1=-1.0, scalar2=0.0, op0=ALU.mult, op1=ALU.add
+            )
+
+        def sum_scalar(i):
+            unused = alternating.tile([P, FEATURES], BF16, tag="unused", name="unused")
+            nc.scalar.activation(out=unused[:], in_=x_tile(i), func=ACT.Identity, accum_out=x_sum[i][:])
+
+        def negate_mean_scalar(i):
+            nc.scalar.mul(out=minus_mean[i][:], in_=x_sum[i][:], mul=-1.0 / FEATURES)
+
+        def squares_scalar(i):
+            unused = alternating.tile([P, FEATURES], BF16, tag="unused", name="unused")
+            nc.scalar.activation(
+                out=unused[:], in_=x_tile(i), func=ACT.Square, bias=minus_mean[i][:], scale=1.0,
+                accum_out=sq_sum[i][:],
+            )
+
+        def root(i):
+            dst = std[i // 2][:, i % 2 : i % 2 + 1]
+            if i in STATS_ON_VECTOR:
+                nc.scalar.activation(out=dst, in_=mean_var[i][:, 1:2], func=ACT.Sqrt, bias=eps[:], scale=1.0)
+            else:
+                nc.scalar.activation(out=dst, in_=sq_sum[i][:], func=ACT.Sqrt, bias=eps[:], scale=1.0 / FEATURES)
+
+        def reciprocal(j):
+            nc.vector.reciprocal(out=rstd[j][:], in_=std[j][:])
+
+        def normalise(i):
+            normalised = normalised_pool.tile([P, 8, P], F32, tag="normalised", name="normalised")
+            live[("normalised", i)] = normalised
+            eng = nc.vector if i in NORMALISE_ON_VECTOR else nc.gpsimd
+            eng.tensor_scalar(
+                out=normalised[:].rearrange("p (g t) q -> p g t q", t=4),
+                in0=x_tile(i).rearrange("p (g q t) -> p g t q", g=2, t=4),
+                scalar1=minus_mean[i][:],
+                scalar2=rstd[i // 2][:, i % 2 : i % 2 + 1],
+                op0=ALU.add,
+                op1=ALU.mult,
+            )
+
+        def transpose_planes(j, g, b):
+            bank = transposes_psum.tile([P, CHUNK], F32, tag="bank", name="plane_bank")
+            live[("plane_bank", j, g, b)] = bank
+            for a in range(2):
+                for n in range(2):
+                    o = 256 * a + P * n
+                    nc.tensor.transpose(
+                        bank[:, o : o + P], live[("normalised", 2 * j + n)][:, 4 * g + 2 * b + a, :], identity[:]
+                    )
+
+        def gain_and_shift(j, g, b):
+            if ("planes", j) not in live:
+                live[("planes", j)] = planes_pool.tile([P, 8, 256], BF16, tag="planes", name="planes")
+            for a in range(2):
+                pl = 4 * g + 2 * b + a
+                nc.scalar.activation(
+                    out=live[("planes", j)][:, pl, :], in_=live[("plane_bank", j, g, b)][:, 256 * a : 256 * a + 256],
+                    func=ACT.Identity, scale=gain_shift[:, pl : pl + 1], bias=gain_shift[:, 8 + pl : 9 + pl],
+                )
+
+        def regroup_planes(j, g):
+            grouped = grouped_pool.tile([P, 256, 4], BF16, tag="grouped", name="grouped", align_bytes=64)
+            live[("grouped", j, g)] = grouped
+            four = live[("planes", j)][:, 4 * g : 4 * g + 4, :]
+            where = regroup_engine(j, g)
+            if where == "G":
+                nc.gpsimd.tensor_scalar(
+                    out=grouped[:], in0=four.rearrange("p t r -> p r t"), scalar1=1.0, scalar2=0.0,
+                    op0=ALU.mult, op1=ALU.add,
+                )
+            else:
+                dst = grouped[:].rearrange("p (c i) t -> p c t i", i=4)
+                src = four.rearrange("p t (c i) -> p c t i", i=4)
+                if where == "S":
+                    nc.scalar.copy(out=dst, in_=src)
+                else:
+                    nc.vector.tensor_copy(out=dst, in_=src)
+
+        def quantise_planes(j, g):
+            nc.vector.quantize_mx(
+                out=x_codes[j][:, g, :].bitcast(FP8X4),
+                scales=x_scales[j][:, g, :],
+                in_=live[("grouped", j, g)][:].rearrange("p r t -> p (r t)"),
+            )
+
+        def multiply(i, c):
+            sums = sums_psum.tile([P, CHUNK], F32, tag="sums", name="sums")
+            live[("sums", i, c)] = sums
+            j, n = i // 2, i % 2
+            for g in range(2):
+                nc.tensor.matmul_mx(
+                    out=sums[:],
+                    lhsT=x_codes[j][:, g, P * n : P * n + P].bitcast(FP8X4),
+                    lhsT_scale=x_scales[j][:, g, P * n : P * n + P],
+                    rhs=w_codes[:, g, CHUNK * c : CHUNK * c + CHUNK].bitcast(FP8X4),
+                    rhs_scale=w_scales[:, g, CHUNK * c : CHUNK * c + CHUNK],
+                    start=(g == 0),
+                    stop=(g == 1),
+                )
+
+        def add_bias(i, c):
+            if ("result", i, c // 2) not in live:
+                live[("result", i, c // 2)] = result_pool.tile([P, 1024], F32, tag="result", name="result")
+            o = CHUNK * (c % 2)
+            nc.vector.tensor_tensor(
+                out=live[("result", i, c // 2)][:, o : o + CHUNK], in0=live[("sums", i, c)][:],
+                in1=bias[:, CHUNK * c : CHUNK * c + CHUNK], op=ALU.add,
+            )
+
+        def store(i, h):
+            nc.sync.dma_start(out=outs[h][P * i : P * i + P, :], in_=live[("result", i, h)][:])
+
+        def store_chunk(i, c):
+            o = CHUNK * (c % 2)
+            nc.sync.dma_start(
+                out=outs[c // 2][P * i : P * i + P, o : o + CHUNK], in_=live[("result", i, c // 2)][:, o : o + CHUNK]
+            )
+
+        load_tokens(0, 0, 1)
+        load_tokens(0, 1, 1)
+        load_weights(0, 0, 2)
+        load_weights(0, 2, 2)
+        load_tokens(1, 0, 2)
+        load_weights(1, 0, 4)
+        load_tokens(2, 0, 2)
+        load_weights(2, 0, 4)
+        load_weights(3, 0, 4)
+        for j in range(3, GROUPS):
+            load_tokens(j, 0, 2)
+        constants_vector()
+        constants_gpsimd()
+        load_gain_shift()
+        constants_scalar()
+        load_bias()
+
+        for i in (0, 1):
+            stats_vector(i)
+        for i in (0, 1):
+            mean_var_vector(i)
+        for i in (0, 1):
+            negate_mean(i)
+        for i in (0, 1):
+            root(i)
+        reciprocal(0)
+        normalise(0)
+        for n in (0, 1):
+            transpose_weights(0, n)
+            regroup_weights(0, n)
+        transpose_gain_shift()
+        keep_gain_shift()
+        normalise(1)
+        for n in (2, 3):
+            transpose_weights(0, n)
+            regroup_weights(0, n)
+        spread_bias(0)
+        keep_bias(0)
+        for i in (2, 3):
+            stats_vector(i)
+        for g in range(2):
+            quantise_weights(0, g)
+
+        for g in range(2):
+            for b in range(2):
+                transpose_planes(0, g, b)
+                gain_and_shift(0, g, b)
+        regroup_planes(0, 0)
+        for i in (2, 3):
+            mean_var_vector(i)
+        for i in (2, 3):
+            negate_mean(i)
+            root(i)
+        quantise_planes(0, 0)
+        stats_vector(4)
+        regroup_planes(0, 1)
+        quantise_planes(0, 1)
+        stats_vector(5)
+        for n in range(4):
+            transpose_weights(1, n)
+            regroup_weights(1, n)
+        reciprocal(1)
+        normalise(2)
+        for g in range(2):
+            quantise_weights(1, g)
+        normalise(3)
+        for i in (4, 5):
+            mean_var_vector(i)
+        for i in (4, 5):
+            negate_mean(i)
+
+        for i in (0, 1):
+            multiply(i, 0)
+            add_bias(i, 0)
+        for n in range(4):
+            transpose_weights(2, n)
+            regroup_weights(2, n)
+        for i in (4, 5):
+            root(i)
+        reciprocal(2)
+        for g in range(2):
+            quantise_weights(2, g)
+        for i in (4, 5):
+            normalise(i)
+        for i in (6, 7):
+            stats_vector(i)
+        for i in (0, 1):
+            multiply(i, 1)
+            add_bias(i, 1)
+            store(i, 0)
+        for i in (6, 7):
+            mean_var_vector(i)
+        stats_vector(8)
+        for g in range(2):
+            for b in range(2):
+                transpose_planes(1, g, b)
+                gain_and_shift(1, g, b)
+        regroup_planes(1, 0)
+        for i in (6, 7):
+            negate_mean(i)
+        for n in range(4):
+            transpose_weights(3, n)
+            regroup_weights(3, n)
+        for g in range(2):
+            quantise_weights(3, g)
+        regroup_planes(1, 1)
+        spread_bias(1)
+        keep_bias(1)
+        for i in (6, 7):
+            root(i)
+        for c in (2, 3):
+            for i in (0, 1):
+                multiply(i, c)
+        add_bias(0, 2)
+        for g in range(2):
+            quantise_planes(1, g)
+        reciprocal(3)
+        add_bias(1, 2)
+        for i in (0, 1):
+            add_bias(i, 3)
+            store(i, 1)
+        stats_vector(9)
+        sum_scalar(10)
+        sum_scalar(11)
+        negate_mean_scalar(10)
+        squares_scalar(10)
+
+        for j in range(1, GROUPS):
+            even, odd = 2 * j, 2 * j + 1
+            ahead = j + 1
+            second = SECOND_PASS.get(j, ())
+            first = FIRST_PASS.get(j, ())
+            if ahead < GROUPS:
+                for g in range(2):
+                    for b in range(2):
+                        transpose_planes(ahead, g, b)
+                gain_and_shift(ahead, 0, 0)
+            for i in second:
+                negate_mean_scalar(i)
+            if ahead < GROUPS:
+                gain_and_shift(ahead, 0, 1)
+                gain_and_shift(ahead, 1, 0)
+                gain_and_shift(ahead, 1, 1)
+            for i in second:
+                squares_scalar(i)
+            if j + 2 < GROUPS:
+                normalise(2 * j + 4)
+                normalise(2 * j + 5)
+            if ahead < GROUPS:
+                regroup_planes(ahead, 0)
+                if regroup_engine(ahead, 1) == "S":
+                    regroup_planes(ahead, 1)
+
+            for c in range(4):
+                multiply(even, c)
+            for c in range(4):
+                add_bias(even, c)
+            store(even, 0)
+            store(even, 1)
+            if j == 1:
+                for i in (8, 9):
+                    mean_var_vector(i)
+                for i in (8, 9):
+                    negate_mean(i)
+                    root(i)
+                root(10)
+            if ahead < GROUPS and regroup_engine(ahead, 1) == "S":
+                for i in second:
+                    root(i)
+                for i in first:
+                    sum_scalar(i)
+            else:
+                for i in first:
+                    sum_scalar(i)
+                for i in second:
+                    root(i)
+
+            for c in range(4):
+                multiply(odd, c)
+            add_bias(odd, 0)
+            add_bias(odd, 1)
+            store(odd, 0)
+            if ahead < GROUPS:
+                if regroup_engine(ahead, 1) == "V":
+                    regroup_planes(ahead, 1)
+                quantise_planes(ahead, 0)
+                quantise_planes(ahead, 1)
+            if j + 3 < GROUPS:
+                reciprocal(j + 3)
+            if odd < TILES - 1:
+                add_bias(odd, 2)
+                add_bias(odd, 3)
+                store(odd, 1)
+            else:
+                for c in (2, 3):
+                    add_bias(odd, c)
+                    store_chunk(odd, c)

@@ -80,8 +80,10 @@ def tile_attentionalpoolerwmasking_pa_kernel(tc, x, ln_k_w, ln_k_b, Wk, Wv, bk, 
         def x_tile(i):
             return x_in[i // 2][:, i % 2, :]
 
-        def constants_vector():
+        def clear_vector_rows():
             nc.vector.memset(vector_rows[:], 0.0)
+
+        def constants_vector():
             nc.vector.memset(zero[:], 0.0)
             nc.vector.tensor_scalar(out=eps[:], in0=zero[:], scalar1=EPS, scalar2=None, op0=ALU.add)
             nc.vector.memset(bias_rows[:], 0.0)
@@ -94,8 +96,8 @@ def tile_attentionalpoolerwmasking_pa_kernel(tc, x, ln_k_w, ln_k_b, Wk, Wv, bk, 
             make_identity(nc, identity[:])
 
         def load_gain_shift():
-            nc.scalar.dma_start(out=vector_rows[0:2, :], in_=ln_k_w.rearrange("(v q) -> v q", v=2))
-            nc.scalar.dma_start(out=vector_rows[2:4, :], in_=ln_k_b.rearrange("(v q) -> v q", v=2))
+            nc.sync.dma_start(out=vector_rows[0:2, :], in_=ln_k_w.rearrange("(v q) -> v q", v=2))
+            nc.sync.dma_start(out=vector_rows[2:4, :], in_=ln_k_b.rearrange("(v q) -> v q", v=2))
 
         def load_bias():
             nc.scalar.dma_start(out=bias_rows[0:1, 0:1024], in_=bk.rearrange("(o d) -> o d", o=1))
@@ -296,6 +298,8 @@ def tile_attentionalpoolerwmasking_pa_kernel(tc, x, ln_k_w, ln_k_b, Wk, Wv, bk, 
                 out=outs[c // 2][P * i : P * i + P, o : o + CHUNK], in_=live[("result", i, c // 2)][:, o : o + CHUNK]
             )
 
+        clear_vector_rows()
+        load_gain_shift()
         load_tokens(0, 0, 1)
         load_tokens(0, 1, 1)
         load_weights(0, 0, 2)
@@ -309,7 +313,6 @@ def tile_attentionalpoolerwmasking_pa_kernel(tc, x, ln_k_w, ln_k_b, Wk, Wv, bk, 
             load_tokens(j, 0, 2)
         constants_vector()
         constants_gpsimd()
-        load_gain_shift()
         constants_scalar()
         load_bias()
 
@@ -326,12 +329,12 @@ def tile_attentionalpoolerwmasking_pa_kernel(tc, x, ln_k_w, ln_k_b, Wk, Wv, bk, 
         for n in (0, 1):
             transpose_weights(0, n)
             regroup_weights(0, n)
-        transpose_gain_shift()
-        keep_gain_shift()
         normalise(1)
         for n in (2, 3):
             transpose_weights(0, n)
             regroup_weights(0, n)
+        transpose_gain_shift()
+        keep_gain_shift()
         spread_bias(0)
         keep_bias(0)
         for i in (2, 3):

@@ -19,7 +19,7 @@ GROUPS = 8
 CHUNK = 512
 FLOPS = 2 * 2048 * 1024 * 2048
 
-PSUM_RING = 4
+PSUM_RING = 8
 NORMALISED_BUFS = 6
 PLANES_BUFS = 3
 GROUPED_BUFS = 4
@@ -50,8 +50,7 @@ def tile_attentionalpoolerwmasking_pa_kernel(tc, x, ln_k_w, ln_k_b, Wk, Wv, bk, 
         planes_pool = ctx.enter_context(tc.tile_pool(name="planes", bufs=PLANES_BUFS))
         grouped_pool = ctx.enter_context(tc.tile_pool(name="grouped", bufs=GROUPED_BUFS))
         result_pool = ctx.enter_context(tc.tile_pool(name="result", bufs=RESULT_BUFS))
-        transposes_psum = ctx.enter_context(tc.psum_pool(name="transposes", bufs=PSUM_RING))
-        sums_psum = ctx.enter_context(tc.psum_pool(name="sums", bufs=PSUM_RING))
+        psum = ctx.enter_context(tc.psum_pool(name="psum", bufs=PSUM_RING))
 
         vector_rows = keep.tile([P, 512], BF16, name="vector_rows")
         bias_rows = keep.tile([P, 2048], BF16, name="bias_rows")
@@ -110,6 +109,12 @@ def tile_attentionalpoolerwmasking_pa_kernel(tc, x, ln_k_w, ln_k_b, Wk, Wv, bk, 
                 in_=tokens[r0 : r0 + P * count, :].rearrange("(n p) c -> p n c", p=P),
             )
 
+        def load_half_tile(i, h):
+            nc.sync.dma_start(
+                out=x_tile(i)[:, 512 * h : 512 * h + 512],
+                in_=tokens[P * i : P * i + P, 512 * h : 512 * h + 512],
+            )
+
         def load_weights(c, n0, count):
             w = Wk if c < 2 else Wv
             r0 = CHUNK * (c % 2) + P * n0
@@ -118,7 +123,7 @@ def tile_attentionalpoolerwmasking_pa_kernel(tc, x, ln_k_w, ln_k_b, Wk, Wv, bk, 
             )
 
         def transpose_gain_shift():
-            bank = transposes_psum.tile([P, CHUNK], F32, tag="bank", name="vector_bank")
+            bank = psum.tile([P, CHUNK], F32, tag="bank", name="vector_bank")
             live["vector_bank"] = bank
             words = vector_rows[:].bitcast(F32)
             for u in range(2):
@@ -131,7 +136,7 @@ def tile_attentionalpoolerwmasking_pa_kernel(tc, x, ln_k_w, ln_k_b, Wk, Wv, bk, 
             )
 
         def spread_bias(h):
-            bank = transposes_psum.tile([P, 1024], BF16, tag="bank", name="bias_bank")
+            bank = psum.tile([P, 1024], BF16, tag="bank", name="bias_bank")
             live[("bias_bank", h)] = bank
             for c in range(2):
                 o = 1024 * h + CHUNK * c
@@ -144,7 +149,7 @@ def tile_attentionalpoolerwmasking_pa_kernel(tc, x, ln_k_w, ln_k_b, Wk, Wv, bk, 
             nc.scalar.copy(out=bias[:, 1024 * h : 1024 * h + 1024], in_=live[("bias_bank", h)][:])
 
         def transpose_weights(c, n):
-            bank = transposes_psum.tile([P, CHUNK], F32, tag="bank", name="weight_bank")
+            bank = psum.tile([P, CHUNK], F32, tag="bank", name="weight_bank")
             live[("weight_bank", c, n)] = bank
             words = w_in[c][:, n, :].bitcast(F32)
             for g in range(2):
@@ -207,6 +212,10 @@ def tile_attentionalpoolerwmasking_pa_kernel(tc, x, ln_k_w, ln_k_b, Wk, Wv, bk, 
         def reciprocal(j):
             nc.vector.reciprocal(out=rstd[j][:], in_=std[j][:])
 
+        def reciprocal_tile(i):
+            n = i % 2
+            nc.vector.reciprocal(out=rstd[i // 2][:, n : n + 1], in_=std[i // 2][:, n : n + 1])
+
         def normalise(i):
             normalised = normalised_pool.tile([P, 8, P], F32, tag="normalised", name="normalised")
             live[("normalised", i)] = normalised
@@ -221,7 +230,7 @@ def tile_attentionalpoolerwmasking_pa_kernel(tc, x, ln_k_w, ln_k_b, Wk, Wv, bk, 
             )
 
         def transpose_planes(j, g, b):
-            bank = transposes_psum.tile([P, CHUNK], F32, tag="bank", name="plane_bank")
+            bank = psum.tile([P, CHUNK], F32, tag="bank", name="plane_bank")
             live[("plane_bank", j, g, b)] = bank
             for a in range(2):
                 for n in range(2):
@@ -266,7 +275,7 @@ def tile_attentionalpoolerwmasking_pa_kernel(tc, x, ln_k_w, ln_k_b, Wk, Wv, bk, 
             )
 
         def multiply(i, c):
-            sums = sums_psum.tile([P, CHUNK], F32, tag="sums", name="sums")
+            sums = psum.tile([P, CHUNK], F32, tag="bank", name="sums")
             live[("sums", i, c)] = sums
             j, n = i // 2, i % 2
             for g in range(2):
@@ -283,25 +292,29 @@ def tile_attentionalpoolerwmasking_pa_kernel(tc, x, ln_k_w, ln_k_b, Wk, Wv, bk, 
         def add_bias(i, c):
             if ("result", i, c // 2) not in live:
                 live[("result", i, c // 2)] = result_pool.tile([P, 1024], F32, tag="result", name="result")
-            o = CHUNK * (c % 2)
+            add_bias_part(i, c, 0, CHUNK)
+
+        def add_bias_part(i, c, f0, count):
+            o = CHUNK * (c % 2) + f0
             nc.vector.tensor_tensor(
-                out=live[("result", i, c // 2)][:, o : o + CHUNK], in0=live[("sums", i, c)][:],
-                in1=bias[:, CHUNK * c : CHUNK * c + CHUNK], op=ALU.add,
+                out=live[("result", i, c // 2)][:, o : o + count], in0=live[("sums", i, c)][:, f0 : f0 + count],
+                in1=bias[:, CHUNK * c + f0 : CHUNK * c + f0 + count], op=ALU.add,
             )
 
         def store(i, h):
             nc.sync.dma_start(out=outs[h][P * i : P * i + P, :], in_=live[("result", i, h)][:])
 
-        def store_chunk(i, c):
-            o = CHUNK * (c % 2)
+        def store_part(i, c, f0, count):
+            o = CHUNK * (c % 2) + f0
             nc.sync.dma_start(
-                out=outs[c // 2][P * i : P * i + P, o : o + CHUNK], in_=live[("result", i, c // 2)][:, o : o + CHUNK]
+                out=outs[c // 2][P * i : P * i + P, o : o + count], in_=live[("result", i, c // 2)][:, o : o + count]
             )
 
         clear_vector_rows()
-        load_gain_shift()
-        load_tokens(0, 0, 1)
+        for h in range(2):
+            load_half_tile(0, h)
         load_tokens(0, 1, 1)
+        load_gain_shift()
         load_weights(0, 0, 2)
         load_weights(0, 2, 2)
         load_tokens(1, 0, 2)
@@ -318,25 +331,17 @@ def tile_attentionalpoolerwmasking_pa_kernel(tc, x, ln_k_w, ln_k_b, Wk, Wv, bk, 
 
         for i in (0, 1):
             stats_vector(i)
-        for i in (0, 1):
             mean_var_vector(i)
-        for i in (0, 1):
             negate_mean(i)
-        for i in (0, 1):
             root(i)
-        reciprocal(0)
-        normalise(0)
-        for n in (0, 1):
-            transpose_weights(0, n)
-            regroup_weights(0, n)
-        normalise(1)
-        for n in (2, 3):
+        for i in (0, 1):
+            reciprocal_tile(i)
+            normalise(i)
+        for n in range(4):
             transpose_weights(0, n)
             regroup_weights(0, n)
         transpose_gain_shift()
         keep_gain_shift()
-        spread_bias(0)
-        keep_bias(0)
         for i in (2, 3):
             stats_vector(i)
         for g in range(2):
@@ -360,6 +365,8 @@ def tile_attentionalpoolerwmasking_pa_kernel(tc, x, ln_k_w, ln_k_b, Wk, Wv, bk, 
         for n in range(4):
             transpose_weights(1, n)
             regroup_weights(1, n)
+        spread_bias(0)
+        keep_bias(0)
         reciprocal(1)
         normalise(2)
         for g in range(2):
@@ -493,6 +500,8 @@ def tile_attentionalpoolerwmasking_pa_kernel(tc, x, ln_k_w, ln_k_b, Wk, Wv, bk, 
                 add_bias(odd, 3)
                 store(odd, 1)
             else:
-                for c in (2, 3):
-                    add_bias(odd, c)
-                    store_chunk(odd, c)
+                add_bias(odd, 2)
+                store_part(odd, 2, 0, CHUNK)
+                for f0 in (0, 256):
+                    add_bias_part(odd, 3, f0, 256)
+                    store_part(odd, 3, f0, 256)

from contextlib import ExitStack

import concourse.mybir as mybir
from concourse.masks import make_identity

F32 = mybir.dt.float32
BF16 = mybir.dt.bfloat16
U32 = mybir.dt.uint32
U8 = mybir.dt.uint8
FP8X4 = mybir.dt.float8_e4m3fn_x4
ALU = mybir.AluOpType
ACT = mybir.ActivationFunctionType

P = 128
FEATURES = 1024
EPS = 1e-5
TILES = 16
GROUPS = 8
CHUNK = 512
FLOPS = 2 * 2048 * 1024 * 2048

PSUM_RING = 8
NORMALISED_BUFS = 6
PLANES_BUFS = 3
GROUPED_BUFS = 4
RESULT_BUFS = 5

STATS_ON_VECTOR = tuple(range(10))
NORMALISE_ON_VECTOR = tuple(range(4))
REGROUP_1_ON_SCALAR = (0, 2, 6, 7)
SECOND_PASS = {1: (11,), 2: (12,), 3: (13,), 4: (14, 15)}
FIRST_PASS = {1: (12,), 2: (13,), 3: (14, 15)}


def regroup_engine(j, g):
    if g == 0:
        return "V" if j == 0 else "G"
    return "S" if j in REGROUP_1_ON_SCALAR else "V"


def tile_attentionalpoolerwmasking_pa_kernel(tc, x, ln_k_w, ln_k_b, Wk, Wv, bk, bv, out_0, out_1):
    nc = tc.nc
    tokens = x.flatten_outer_dims()
    outs = (out_0.flatten_outer_dims(), out_1.flatten_outer_dims())
    with ExitStack() as ctx:
        ctx.enter_context(tc.manual_schedule())
        keep = ctx.enter_context(tc.tile_pool(name="keep", bufs=1))
        normalised_pool = ctx.enter_context(tc.tile_pool(name="normalised", bufs=NORMALISED_BUFS))
        alternating = ctx.enter_context(tc.tile_pool(name="alternating", bufs=2))
        planes_pool = ctx.enter_context(tc.tile_pool(name="planes", bufs=PLANES_BUFS))
        grouped_pool = ctx.enter_context(tc.tile_pool(name="grouped", bufs=GROUPED_BUFS))
        result_pool = ctx.enter_context(tc.tile_pool(name="result", bufs=RESULT_BUFS))
        psum = ctx.enter_context(tc.psum_pool(name="psum", bufs=PSUM_RING))

        vector_rows = keep.tile([P, 512], BF16, name="vector_rows")
        bias_rows = keep.tile([P, 2048], BF16, name="bias_rows")
        ones = keep.tile([P, P], BF16, name="ones")
        zero = keep.tile([P, 1], F32, name="zero")
        eps = keep.tile([P, 1], F32, name="eps")
        warm = keep.tile([P, 1], F32, name="warm")
        identity = keep.tile([P, P], F32, name="identity")
        gain_shift = keep.tile([P, 16], F32, name="gain_shift")
        bias = keep.tile([P, 2048], BF16, name="bias")
        x_in = [keep.tile([P, 2, FEATURES], BF16, name="x_in%d" % j) for j in range(GROUPS)]
        w_in = [keep.tile([P, 4, FEATURES], BF16, name="w_in%d" % c) for c in range(4)]
        w_codes = keep.tile([P, 2, 2048], U32, name="w_codes", align_bytes=64)
        w_scales = keep.tile([P, 2, 2048], U8, name="w_scales", align_bytes=64)
        x_codes = [keep.tile([P, 2, 256], U32, name="x_codes%d" % j, align_bytes=64) for j in range(GROUPS)]
        x_scales = [keep.tile([P, 2, 256], U8, name="x_scales%d" % j, align_bytes=64) for j in range(GROUPS)]
        chunk_stats = {i: keep.tile([P, 2, 6], F32, name="chunk_stats%d" % i) for i in STATS_ON_VECTOR}
        mean_var = {i: keep.tile([P, 2], F32, name="mean_var%d" % i) for i in STATS_ON_VECTOR}
        x_sum = {i: keep.tile([P, 1], F32, name="x_sum%d" % i) for i in range(TILES) if i not in STATS_ON_VECTOR}
        sq_sum = {i: keep.tile([P, 1], F32, name="sq_sum%d" % i) for i in range(TILES) if i not in STATS_ON_VECTOR}
        minus_mean = [keep.tile([P, 1], F32, name="minus_mean%d" % i) for i in range(TILES)]
        std = [keep.tile([P, 2], F32, name="std%d" % j) for j in range(GROUPS)]
        rstd = [keep.tile([P, 2], F32, name="rstd%d" % j) for j in range(GROUPS)]
        live = {}

        def x_tile(i):
            return x_in[i // 2][:, i % 2, :]

        def clear_vector_rows():
            nc.vector.memset(vector_rows[:], 0.0)

        def constants_vector():
            nc.vector.memset(zero[:], 0.0)
            nc.vector.tensor_scalar(out=eps[:], in0=zero[:], scalar1=EPS, scalar2=None, op0=ALU.add)
            nc.vector.memset(bias_rows[:], 0.0)
            nc.vector.memset(ones[:], 1.0)

        def constants_scalar():
            nc.scalar.activation(out=warm[:], in_=eps[:], func=ACT.Sqrt)

        def constants_gpsimd():
            make_identity(nc, identity[:])

        def load_gain_shift():
            nc.sync.dma_start(out=vector_rows[0:2, :], in_=ln_k_w.rearrange("(v q) -> v q", v=2))
            nc.sync.dma_start(out=vector_rows[2:4, :], in_=ln_k_b.rearrange("(v q) -> v q", v=2))

        def load_bias():
            nc.scalar.dma_start(out=bias_rows[0:1, 0:1024], in_=bk.rearrange("(o d) -> o d", o=1))
            nc.scalar.dma_start(out=bias_rows[0:1, 1024:2048], in_=bv.rearrange("(o d) -> o d", o=1))

        def load_tokens(j, n0, count):
            r0 = P * (2 * j + n0)
            nc.sync.dma_start(
                out=x_in[j][:, n0 : n0 + count, :],
                in_=tokens[r0 : r0 + P * count, :].rearrange("(n p) c -> p n c", p=P),
            )

        def load_half_tile(i, h):
            nc.sync.dma_start(
                out=x_tile(i)[:, 512 * h : 512 * h + 512],
                in_=tokens[P * i : P * i + P, 512 * h : 512 * h + 512],
            )

        def load_weights(c, n0, count):
            w = Wk if c < 2 else Wv
            r0 = CHUNK * (c % 2) + P * n0
            nc.sync.dma_start(
                out=w_in[c][:, n0 : n0 + count, :], in_=w[r0 : r0 + P * count, :].rearrange("(n p) c -> p n c", p=P)
            )

        def transpose_gain_shift():
            bank = psum.tile([P, CHUNK], F32, tag="bank", name="vector_bank")
            live["vector_bank"] = bank
            words = vector_rows[:].bitcast(F32)
            for u in range(2):
                nc.tensor.transpose(bank[:, P * u : P * u + P], words[:, u : 256 : 2], identity[:])

        def keep_gain_shift():
            nc.vector.tensor_copy(
                out=gain_shift[:].rearrange("p (r u e) -> p r u e", u=2, e=2),
                in_=live["vector_bank"][:, 0:256].bitcast(BF16).rearrange("p (u r e) -> p r u e", u=2, e=2)[:, 0:4, :, :],
            )

        def spread_bias(h):
            bank = psum.tile([P, 1024], BF16, tag="bank", name="bias_bank")
            live[("bias_bank", h)] = bank
            for c in range(2):
                o = 1024 * h + CHUNK * c
                nc.tensor.matmul(
                    out=bank[:, CHUNK * c : CHUNK * c + CHUNK], lhsT=ones[:], rhs=bias_rows[:, o : o + CHUNK],
                    start=True, stop=True,
                )

        def keep_bias(h):
            nc.scalar.copy(out=bias[:, 1024 * h : 1024 * h + 1024], in_=live[("bias_bank", h)][:])

        def transpose_weights(c, n):
            bank = psum.tile([P, CHUNK], F32, tag="bank", name="weight_bank")
            live[("weight_bank", c, n)] = bank
            words = w_in[c][:, n, :].bitcast(F32)
            for g in range(2):
                for u in range(2):
                    o = 256 * g + P * u
                    nc.tensor.transpose(bank[:, o : o + P], words[:, 256 * g + u : 256 * g + 256 : 2], identity[:])

        def regroup_weights(c, n):
            if ("weight_pairs", c) not in live:
                live[("weight_pairs", c)] = alternating.tile(
                    [P, 2, 2048], BF16, tag="weight_pairs", name="weight_pairs", align_bytes=64
                )
            words = live[("weight_pairs", c)][:].bitcast(F32).rearrange("p g (d u) -> p g d u", u=2)
            nc.scalar.copy(
                out=words[:, :, P * n : P * n + P, :],
                in_=live[("weight_bank", c, n)][:].rearrange("p (g u d) -> p g d u", g=2, u=2),
            )

        def quantise_weights(c, g):
            nc.vector.quantize_mx(
                out=w_codes[:, g, CHUNK * c : CHUNK * c + CHUNK].bitcast(FP8X4),
                scales=w_scales[:, g, CHUNK * c : CHUNK * c + CHUNK],
                in_=live[("weight_pairs", c)][:, g, :],
            )

        def stats_vector(i):
            for h in range(2):
                nc.vector.bn_stats(out=chunk_stats[i][:, h, :], in_=x_tile(i)[:, 512 * h : 512 * h + 512])

        def mean_var_vector(i):
            nc.vector.bn_aggr(out=mean_var[i][:], in_=chunk_stats[i][:].rearrange("p a b -> p (a b)"))

        def negate_mean(i):
            eng = nc.vector if i in NORMALISE_ON_VECTOR else nc.gpsimd
            eng.tensor_scalar(
                out=minus_mean[i][:], in0=mean_var[i][:, 0:1], scalar1=-1.0, scalar2=0.0, op0=ALU.mult, op1=ALU.add
            )

        def sum_scalar(i):
            unused = alternating.tile([P, FEATURES], BF16, tag="unused", name="unused")
            nc.scalar.activation(out=unused[:], in_=x_tile(i), func=ACT.Identity, accum_out=x_sum[i][:])

        def negate_mean_scalar(i):
            nc.scalar.mul(out=minus_mean[i][:], in_=x_sum[i][:], mul=-1.0 / FEATURES)

        def squares_scalar(i):
            unused = alternating.tile([P, FEATURES], BF16, tag="unused", name="unused")
            nc.scalar.activation(
                out=unused[:], in_=x_tile(i), func=ACT.Square, bias=minus_mean[i][:], scale=1.0,
                accum_out=sq_sum[i][:],
            )

        def root(i):
            dst = std[i // 2][:, i % 2 : i % 2 + 1]
            if i in STATS_ON_VECTOR:
                nc.scalar.activation(out=dst, in_=mean_var[i][:, 1:2], func=ACT.Sqrt, bias=eps[:], scale=1.0)
            else:
                nc.scalar.activation(out=dst, in_=sq_sum[i][:], func=ACT.Sqrt, bias=eps[:], scale=1.0 / FEATURES)

        def reciprocal(j):
            nc.vector.reciprocal(out=rstd[j][:], in_=std[j][:])

        def reciprocal_tile(i):
            n = i % 2
            nc.vector.reciprocal(out=rstd[i // 2][:, n : n + 1], in_=std[i // 2][:, n : n + 1])

        def normalise(i):
            normalised = normalised_pool.tile([P, 8, P], F32, tag="normalised", name="normalised")
            live[("normalised", i)] = normalised
            eng = nc.vector if i in NORMALISE_ON_VECTOR else nc.gpsimd
            eng.tensor_scalar(
                out=normalised[:].rearrange("p (g t) q -> p g t q", t=4),
                in0=x_tile(i).rearrange("p (g q t) -> p g t q", g=2, t=4),
                scalar1=minus_mean[i][:],
                scalar2=rstd[i // 2][:, i % 2 : i % 2 + 1],
                op0=ALU.add,
                op1=ALU.mult,
            )

        def transpose_planes(j, g, b):
            bank = psum.tile([P, CHUNK], F32, tag="bank", name="plane_bank")
            live[("plane_bank", j, g, b)] = bank
            for a in range(2):
                for n in range(2):
                    o = 256 * a + P * n
                    nc.tensor.transpose(
                        bank[:, o : o + P], live[("normalised", 2 * j + n)][:, 4 * g + 2 * b + a, :], identity[:]
                    )

        def gain_and_shift(j, g, b):
            if ("planes", j) not in live:
                live[("planes", j)] = planes_pool.tile([P, 8, 256], BF16, tag="planes", name="planes")
            for a in range(2):
                pl = 4 * g + 2 * b + a
                nc.scalar.activation(
                    out=live[("planes", j)][:, pl, :], in_=live[("plane_bank", j, g, b)][:, 256 * a : 256 * a + 256],
                    func=ACT.Identity, scale=gain_shift[:, pl : pl + 1], bias=gain_shift[:, 8 + pl : 9 + pl],
                )

        def regroup_planes(j, g):
            grouped = grouped_pool.tile([P, 256, 4], BF16, tag="grouped", name="grouped", align_bytes=64)
            live[("grouped", j, g)] = grouped
            four = live[("planes", j)][:, 4 * g : 4 * g + 4, :]
            where = regroup_engine(j, g)
            if where == "G":
                nc.gpsimd.tensor_scalar(
                    out=grouped[:], in0=four.rearrange("p t r -> p r t"), scalar1=1.0, scalar2=0.0,
                    op0=ALU.mult, op1=ALU.add,
                )
            else:
                dst = grouped[:].rearrange("p (c i) t -> p c t i", i=4)
                src = four.rearrange("p t (c i) -> p c t i", i=4)
                if where == "S":
                    nc.scalar.copy(out=dst, in_=src)
                else:
                    nc.vector.tensor_copy(out=dst, in_=src)

        def quantise_planes(j, g):
            nc.vector.quantize_mx(
                out=x_codes[j][:, g, :].bitcast(FP8X4),
                scales=x_scales[j][:, g, :],
                in_=live[("grouped", j, g)][:].rearrange("p r t -> p (r t)"),
            )

        def multiply(i, c):
            sums = psum.tile([P, CHUNK], F32, tag="bank", name="sums")
            live[("sums", i, c)] = sums
            j, n = i // 2, i % 2
            for g in range(2):
                nc.tensor.matmul_mx(
                    out=sums[:],
                    lhsT=x_codes[j][:, g, P * n : P * n + P].bitcast(FP8X4),
                    lhsT_scale=x_scales[j][:, g, P * n : P * n + P],
                    rhs=w_codes[:, g, CHUNK * c : CHUNK * c + CHUNK].bitcast(FP8X4),
                    rhs_scale=w_scales[:, g, CHUNK * c : CHUNK * c + CHUNK],
                    start=(g == 0),
                    stop=(g == 1),
                )

        def add_bias(i, c):
            if ("result", i, c // 2) not in live:
                live[("result", i, c // 2)] = result_pool.tile([P, 1024], F32, tag="result", name="result")
            add_bias_part(i, c, 0, CHUNK)

        def add_bias_part(i, c, f0, count):
            o = CHUNK * (c % 2) + f0
            nc.vector.tensor_tensor(
                out=live[("result", i, c // 2)][:, o : o + count], in0=live[("sums", i, c)][:, f0 : f0 + count],
                in1=bias[:, CHUNK * c + f0 : CHUNK * c + f0 + count], op=ALU.add,
            )

        def store(i, h):
            nc.sync.dma_start(out=outs[h][P * i : P * i + P, :], in_=live[("result", i, h)][:])

        def store_part(i, c, f0, count):
            o = CHUNK * (c % 2) + f0
            nc.sync.dma_start(
                out=outs[c // 2][P * i : P * i + P, o : o + count], in_=live[("result", i, c // 2)][:, o : o + count]
            )

        clear_vector_rows()
        for h in range(2):
            load_half_tile(0, h)
        load_tokens(0, 1, 1)
        load_gain_shift()
        load_weights(0, 0, 2)
        load_weights(0, 2, 2)
        load_tokens(1, 0, 2)
        load_weights(1, 0, 4)
        load_tokens(2, 0, 2)
        load_weights(2, 0, 4)
        load_weights(3, 0, 4)
        for j in range(3, GROUPS):
            load_tokens(j, 0, 2)
        constants_vector()
        constants_gpsimd()
        constants_scalar()
        load_bias()

        for i in (0, 1):
            stats_vector(i)
            mean_var_vector(i)
            negate_mean(i)
            root(i)
        for i in (0, 1):
            reciprocal_tile(i)
            normalise(i)
        for n in range(4):
            transpose_weights(0, n)
            regroup_weights(0, n)
        transpose_gain_shift()
        keep_gain_shift()
        for i in (2, 3):
            stats_vector(i)
        for g in range(2):
            quantise_weights(0, g)

        for g in range(2):
            for b in range(2):
                transpose_planes(0, g, b)
                gain_and_shift(0, g, b)
        regroup_planes(0, 0)
        for i in (2, 3):
            mean_var_vector(i)
        for i in (2, 3):
            negate_mean(i)
            root(i)
        quantise_planes(0, 0)
        stats_vector(4)
        regroup_planes(0, 1)
        quantise_planes(0, 1)
        stats_vector(5)
        for n in range(4):
            transpose_weights(1, n)
            regroup_weights(1, n)
        spread_bias(0)
        keep_bias(0)
        reciprocal(1)
        normalise(2)
        for g in range(2):
            quantise_weights(1, g)
        normalise(3)
        for i in (4, 5):
            mean_var_vector(i)
        for i in (4, 5):
            negate_mean(i)

        for i in (0, 1):
            multiply(i, 0)
            add_bias(i, 0)
        for n in range(4):
            transpose_weights(2, n)
            regroup_weights(2, n)
        for i in (4, 5):
            root(i)
        reciprocal(2)
        for g in range(2):
            quantise_weights(2, g)
        for i in (4, 5):
            normalise(i)
        for i in (6, 7):
            stats_vector(i)
        for i in (0, 1):
            multiply(i, 1)
            add_bias(i, 1)
            store(i, 0)
        for i in (6, 7):
            mean_var_vector(i)
        stats_vector(8)
        for g in range(2):
            for b in range(2):
                transpose_planes(1, g, b)
                gain_and_shift(1, g, b)
        regroup_planes(1, 0)
        for i in (6, 7):
            negate_mean(i)
        for n in range(4):
            transpose_weights(3, n)
            regroup_weights(3, n)
        for g in range(2):
            quantise_weights(3, g)
        regroup_planes(1, 1)
        spread_bias(1)
        keep_bias(1)
        for i in (6, 7):
            root(i)
        for c in (2, 3):
            for i in (0, 1):
                multiply(i, c)
        add_bias(0, 2)
        for g in range(2):
            quantise_planes(1, g)
        reciprocal(3)
        add_bias(1, 2)
        for i in (0, 1):
            add_bias(i, 3)
            store(i, 1)
        stats_vector(9)
        sum_scalar(10)
        sum_scalar(11)
        negate_mean_scalar(10)
        squares_scalar(10)

        for j in range(1, GROUPS):
            even, odd = 2 * j, 2 * j + 1
            ahead = j + 1
            second = SECOND_PASS.get(j, ())
            first = FIRST_PASS.get(j, ())
            if ahead < GROUPS:
                for g in range(2):
                    for b in range(2):
                        transpose_planes(ahead, g, b)
                gain_and_shift(ahead, 0, 0)
            for i in second:
                negate_mean_scalar(i)
            if ahead < GROUPS:
                gain_and_shift(ahead, 0, 1)
                gain_and_shift(ahead, 1, 0)
                gain_and_shift(ahead, 1, 1)
            for i in second:
                squares_scalar(i)
            if j + 2 < GROUPS:
                normalise(2 * j + 4)
                normalise(2 * j + 5)
            if ahead < GROUPS:
                regroup_planes(ahead, 0)
                if regroup_engine(ahead, 1) == "S":
                    regroup_planes(ahead, 1)

            for c in range(4):
                multiply(even, c)
            for c in range(4):
                add_bias(even, c)
            store(even, 0)
            store(even, 1)
            if j == 1:
                for i in (8, 9):
                    mean_var_vector(i)
                for i in (8, 9):
                    negate_mean(i)
                    root(i)
                root(10)
            if ahead < GROUPS and regroup_engine(ahead, 1) == "S":
                for i in second:
                    root(i)
                for i in first:
                    sum_scalar(i)
            else:
                for i in first:
                    sum_scalar(i)
                for i in second:
                    root(i)

            for c in range(4):
                multiply(odd, c)
            add_bias(odd, 0)
            add_bias(odd, 1)
            store(odd, 0)
            if ahead < GROUPS:
                if regroup_engine(ahead, 1) == "V":
                    regroup_planes(ahead, 1)
                quantise_planes(ahead, 0)
                quantise_planes(ahead, 1)
            if j + 3 < GROUPS:
                reciprocal(j + 3)
            if odd < TILES - 1:
                add_bias(odd, 2)
                add_bias(odd, 3)
                store(odd, 1)
            else:
                add_bias(odd, 2)
                store_part(odd, 2, 0, CHUNK)
                for f0 in (0, 256):
                    add_bias_part(odd, 3, f0, 256)
                    store_part(odd, 3, f0, 256)
